import numpy as np
import ml_dtypes


def mxq(x, axis, fmt="e4m3"):
    dtype, down = {"e4m3": (ml_dtypes.float8_e4m3fn, 7), "e5m2": (ml_dtypes.float8_e5m2, 14)}[fmt]
    v = np.moveaxis(np.asarray(x, np.float32).astype(ml_dtypes.bfloat16).astype(np.float64), axis, -1)
    blocks = v.reshape(v.shape[:-1] + (-1, 32))
    amax = np.abs(blocks).max(-1, keepdims=True)
    byte = np.maximum(np.where(amax > 0, np.frexp(amax)[1] - 1 + 127, 0) - down, 1)
    scale = np.exp2(byte - 127.0)
    codes = (blocks / scale).astype(np.float32).astype(dtype).astype(np.float64)
    return np.moveaxis((codes * scale).reshape(v.shape), -1, axis)


WIDE = False


def mx_kscale(k):
    if not WIDE:
        return np.ones(k)
    levels = np.array([10, -10, 5, -5, 0])
    if k % 512:
        return np.exp2(np.random.permutation(np.resize(levels, k // 32))).repeat(32)
    a = np.empty((k // 512, 16))
    for p in range(k // 512):
        a[p, :8] = np.random.permutation(np.resize(levels, 8))
        for g in range(8):
            far = levels[np.abs(levels - a[p, g]) >= 10]
            a[p, g + 8] = far[np.random.randint(len(far))]
    return np.exp2(a.ravel()).repeat(32)


BF16 = ml_dtypes.bfloat16


def bf(x):
    return np.asarray(x, np.float32).astype(BF16)


def f64(x):
    return np.asarray(x).astype(np.float64)


B, J, I, O = 512, 2, 512, 128
IN_CH = J * I
OUT_CH = J * O
NEIGHBOUR_LIST = [[j for j in (i - 1, i, i + 1) if 0 <= j < J] for i in range(J)]


def build_mask():
    mask = np.zeros((OUT_CH, IN_CH))
    for i, neigh in enumerate(NEIGHBOUR_LIST):
        mask[i * O:(i + 1) * O, neigh[0] * I:(neigh[-1] + 1) * I] = 1.0
    return mask


def setup_inputs():
    s = mx_kscale(IN_CH)
    keep = np.random.random((OUT_CH, IN_CH)) < 0.75
    return {"x": bf(np.random.standard_normal((B, IN_CH)) * s),
            "weight": bf(np.random.standard_normal((OUT_CH, IN_CH)) / np.sqrt(0.75 * 3 * I) / s[None, :]),
            "mask": bf(build_mask() * keep),
            "bias": bf(np.random.standard_normal(OUT_CH) * 0.5)}


def reference(x, weight, mask, bias):
    x2 = f64(x).reshape(x.shape[0], -1)
    w = f64(weight) * f64(mask)
    xq = mxq(x2, 1, "e4m3")
    cols = []
    for i, neigh in enumerate(NEIGHBOUR_LIST):
        lo, hi = neigh[0] * I, (neigh[-1] + 1) * I
        cols.append(xq[:, lo:hi] @ mxq(w[i * O:(i + 1) * O, lo:hi], 1, "e4m3").T)
    return np.concatenate(cols, axis=1) + f64(bias)

@@ -1,0 +1,135 @@
+from contextlib import ExitStack
+
+import concourse.mybir as mybir
+from concourse.masks import make_identity
+
+F32 = mybir.dt.float32
+BF16 = mybir.dt.bfloat16
+U32 = mybir.dt.uint32
+U8 = mybir.dt.uint8
+FP8X4 = mybir.dt.float8_e4m3fn_x4
+
+P = 128
+PACK = 4
+K_PASS = P * PACK
+HALVES = 2
+
+B, K, O = 512, 1024, 256
+PASSES = K // K_PASS
+B_TILES = B // P
+O_TILES = O // P
+
+FLOPS = 2 * B * K * O
+
+
+def load_rows(nc, loads, source):
+    rows = loads.tile([P, K], BF16)
+    nc.sync.dma_start(out=rows[:], in_=source)
+    return rows
+
+
+def transpose_and_regroup(nc, banks, rows, identity, grouped):
+    words = rows.bitcast(F32)
+    bank = banks.tile([P, PASSES, HALVES, P], F32)
+    for g in range(PASSES):
+        for u in range(HALVES):
+            every_second = slice(g * HALVES * P + u, (g + 1) * HALVES * P, HALVES)
+            nc.tensor.transpose(bank[:, g, u, :], words[:, every_second], identity)
+    nc.scalar.copy(out=grouped, in_=bank[:].rearrange("p g u c -> p g c u"))
+
+
+def word_view(grouped):
+    return grouped.bitcast(F32).rearrange("p (g c u) -> p g c u", g=PASSES, u=HALVES)
+
+
+def quantise(nc, pool, grouped, rows):
+    codes = pool.tile([P, PASSES, rows], U32, align_bytes=64)
+    scales = pool.tile([P, PASSES, rows], U8, align_bytes=64)
+    nc.vector.quantize_mx(
+        out=codes[:].rearrange("p g c -> p (g c)").bitcast(FP8X4),
+        scales=scales[:].rearrange("p g c -> p (g c)"),
+        in_=grouped,
+    )
+    return codes, scales
+
+
+def tile_skeletonlinear_s_kernel(tc, x, weight, mask, bias, out):
+    nc = tc.nc
+    x_tiles = x.rearrange("(p t) k -> t p k", t=B_TILES)
+    out_tiles = out.rearrange("(p t) o -> t p o", t=B_TILES)
+    weight_tiles = weight.rearrange("(j p) k -> j p k", p=P)
+    mask_tiles = mask.rearrange("(j p) k -> j p k", p=P)
+
+    with ExitStack() as ctx:
+        keep = ctx.enter_context(tc.tile_pool(name="keep", bufs=1))
+        loads = ctx.enter_context(tc.tile_pool(name="loads", bufs=B_TILES + 2 * O_TILES))
+        w_pool = ctx.enter_context(tc.tile_pool(name="w_pool", bufs=O_TILES))
+        x_pool = ctx.enter_context(tc.tile_pool(name="x_pool", bufs=B_TILES))
+        banks = ctx.enter_context(tc.psum_pool(name="banks", bufs=4))
+        sums = ctx.enter_context(tc.psum_pool(name="sums", bufs=4))
+        ctx.enter_context(tc.manual_schedule())
+
+        bias_rows = keep.tile([P, O], BF16)
+        nc.vector.memset(bias_rows[:], 0.0)
+        ones = keep.tile([P, P], BF16)
+        nc.vector.memset(ones[:], 1.0)
+        identity = keep.tile([P, P], F32)
+        make_identity(nc, identity[:])
+
+        x_rows = [load_rows(nc, loads, x_tiles[0])]
+        nc.sync.dma_start(out=bias_rows[0:1, :], in_=bias.unsqueeze(0))
+        weight_rows = []
+        mask_rows = []
+        for j in range(O_TILES):
+            weight_rows.append(load_rows(nc, loads, weight_tiles[j]))
+            mask_rows.append(load_rows(nc, loads, mask_tiles[j]))
+        for t in range(1, B_TILES):
+            x_rows.append(load_rows(nc, loads, x_tiles[t]))
+
+        x_grouped = []
+        for t in range(B_TILES):
+            grouped_t = x_pool.tile([P, PASSES * P * PACK], BF16, align_bytes=64)
+            x_grouped.append(grouped_t)
+        w_grouped = keep.tile([P, PASSES * O * PACK], BF16, align_bytes=64)
+
+        def masked_weight_tile(j):
+            w_j = w_pool.tile([P, K], BF16)
+            for g in range(PASSES):
+                k_pass = slice(g * K_PASS, (g + 1) * K_PASS)
+                nc.vector.tensor_mul(
+                    out=w_j[:, k_pass], in0=weight_rows[j][:, k_pass], in1=mask_rows[j][:, k_pass]
+                )
+            transpose_and_regroup(
+                nc, banks, w_j[:], identity[:], word_view(w_grouped[:])[:, :, j * P : (j + 1) * P, :]
+            )
+
+        transpose_and_regroup(nc, banks, x_rows[0][:], identity[:], word_view(x_grouped[0][:]))
+        masked_weight_tile(0)
+        bias_sum = sums.tile([P, O], F32, tag="sum")
+        nc.tensor.matmul(out=bias_sum[:], lhsT=ones[:], rhs=bias_rows[:], start=True, stop=True)
+        bias_all = keep.tile([P, O], F32)
+        nc.scalar.copy(out=bias_all[:], in_=bias_sum[:])
+        masked_weight_tile(1)
+
+        x_mx = [quantise(nc, x_pool, x_grouped[0][:], P)]
+        w_codes, w_scales = quantise(nc, keep, w_grouped[:], O)
+        for t in range(1, B_TILES):
+            transpose_and_regroup(nc, banks, x_rows[t][:], identity[:], word_view(x_grouped[t][:]))
+            x_mx.append(quantise(nc, x_pool, x_grouped[t][:], P))
+
+        for t in range(B_TILES):
+            x_codes, x_scales = x_mx[t]
+            acc = sums.tile([P, O], F32, tag="sum")
+            for g in range(PASSES):
+                nc.tensor.matmul_mx(
+                    out=acc[:],
+                    lhsT=x_codes[:, g, :].bitcast(FP8X4),
+                    lhsT_scale=x_scales[:, g, :],
+                    rhs=w_codes[:, g, :].bitcast(FP8X4),
+                    rhs_scale=w_scales[:, g, :],
+                    start=(g == 0),
+                    stop=(g == PASSES - 1),
+                )
+            result = x_pool.tile([P, O], F32)
+            nc.vector.tensor_add(out=result[:], in0=acc[:], in1=bias_all[:])
+            nc.sync.dma_start(out=out_tiles[t], in_=result[:])

@@ -22,37 +22,6 @@ O_TILES = O // P
 FLOPS = 2 * B * K * O
 
 
-def load_rows(nc, loads, source):
-    rows = loads.tile([P, K], BF16)
-    nc.sync.dma_start(out=rows[:], in_=source)
-    return rows
-
-
-def transpose_and_regroup(nc, banks, rows, identity, grouped):
-    words = rows.bitcast(F32)
-    bank = banks.tile([P, PASSES, HALVES, P], F32)
-    for g in range(PASSES):
-        for u in range(HALVES):
-            every_second = slice(g * HALVES * P + u, (g + 1) * HALVES * P, HALVES)
-            nc.tensor.transpose(bank[:, g, u, :], words[:, every_second], identity)
-    nc.scalar.copy(out=grouped, in_=bank[:].rearrange("p g u c -> p g c u"))
-
-
-def word_view(grouped):
-    return grouped.bitcast(F32).rearrange("p (g c u) -> p g c u", g=PASSES, u=HALVES)
-
-
-def quantise(nc, pool, grouped, rows):
-    codes = pool.tile([P, PASSES, rows], U32, align_bytes=64)
-    scales = pool.tile([P, PASSES, rows], U8, align_bytes=64)
-    nc.vector.quantize_mx(
-        out=codes[:].rearrange("p g c -> p (g c)").bitcast(FP8X4),
-        scales=scales[:].rearrange("p g c -> p (g c)"),
-        in_=grouped,
-    )
-    return codes, scales
-
-
 def tile_skeletonlinear_s_kernel(tc, x, weight, mask, bias, out):
     nc = tc.nc
     x_tiles = x.rearrange("(p t) k -> t p k", t=B_TILES)
@@ -62,11 +31,9 @@ def tile_skeletonlinear_s_kernel(tc, x, weight, mask, bias, out):
 
     with ExitStack() as ctx:
         keep = ctx.enter_context(tc.tile_pool(name="keep", bufs=1))
-        loads = ctx.enter_context(tc.tile_pool(name="loads", bufs=B_TILES + 2 * O_TILES))
-        w_pool = ctx.enter_context(tc.tile_pool(name="w_pool", bufs=O_TILES))
-        x_pool = ctx.enter_context(tc.tile_pool(name="x_pool", bufs=B_TILES))
-        banks = ctx.enter_context(tc.psum_pool(name="banks", bufs=4))
-        sums = ctx.enter_context(tc.psum_pool(name="sums", bufs=4))
+        loads = ctx.enter_context(tc.tile_pool(name="loads", bufs=1))
+        banks = ctx.enter_context(tc.psum_pool(name="banks", bufs=5))
+        sums = ctx.enter_context(tc.psum_pool(name="sums", bufs=1))
         ctx.enter_context(tc.manual_schedule())
 
         bias_rows = keep.tile([P, O], BF16)
@@ -76,60 +43,140 @@ def tile_skeletonlinear_s_kernel(tc, x, weight, mask, bias, out):
         identity = keep.tile([P, P], F32)
         make_identity(nc, identity[:])
 
-        x_rows = [load_rows(nc, loads, x_tiles[0])]
-        nc.sync.dma_start(out=bias_rows[0:1, :], in_=bias.unsqueeze(0))
-        weight_rows = []
-        mask_rows = []
+        def load(source, label):
+            rows = loads.tile([P, source.shape[1]], BF16, name=label)
+            nc.sync.dma_start(out=rows[:], in_=source)
+            return rows
+
+        x_rows = {t: load(x_tiles[t], f"x{t}") for t in (0, 1)}
+        weight_rows = {}
+        mask_rows = {}
         for j in range(O_TILES):
-            weight_rows.append(load_rows(nc, loads, weight_tiles[j]))
-            mask_rows.append(load_rows(nc, loads, mask_tiles[j]))
-        for t in range(1, B_TILES):
-            x_rows.append(load_rows(nc, loads, x_tiles[t]))
+            weight_rows[j] = load(weight_tiles[j], f"weight{j}")
+            mask_rows[j] = load(mask_tiles[j], f"mask{j}")
+        x_rows[2] = load(x_tiles[2], "x2")
+        last_rows = [load(x_tiles[3][:, g * K_PASS : (g + 1) * K_PASS], f"last{g}") for g in range(PASSES)]
+        nc.scalar.dma_start(out=bias_rows[0:1, :], in_=bias.unsqueeze(0))
 
-        x_grouped = []
+        x_grouped = {}
+        x_codes = {}
+        x_scales = {}
         for t in range(B_TILES):
-            grouped_t = x_pool.tile([P, PASSES * P * PACK], BF16, align_bytes=64)
-            x_grouped.append(grouped_t)
-        w_grouped = keep.tile([P, PASSES * O * PACK], BF16, align_bytes=64)
+            x_grouped[t] = keep.tile([P, PASSES * P * PACK], BF16, align_bytes=64, name=f"x_grouped{t}")
+            x_codes[t] = keep.tile([P, PASSES, P], U32, align_bytes=64, name=f"x_codes{t}")
+            x_scales[t] = keep.tile([P, PASSES, P], U8, align_bytes=64, name=f"x_scales{t}")
+        w_codes = keep.tile([P, PASSES, O], U32, align_bytes=64)
+        w_scales = keep.tile([P, PASSES, O], U8, align_bytes=64)
 
-        def masked_weight_tile(j):
-            w_j = w_pool.tile([P, K], BF16)
-            for g in range(PASSES):
-                k_pass = slice(g * K_PASS, (g + 1) * K_PASS)
-                nc.vector.tensor_mul(
-                    out=w_j[:, k_pass], in0=weight_rows[j][:, k_pass], in1=mask_rows[j][:, k_pass]
-                )
-            transpose_and_regroup(
-                nc, banks, w_j[:], identity[:], word_view(w_grouped[:])[:, :, j * P : (j + 1) * P, :]
+        def transpose_words(words, squares):
+            bank = banks.tile([P, squares // HALVES, HALVES, P], F32, tag="bank")
+            for s in range(squares):
+                g, u = divmod(s, HALVES)
+                every_second = slice(g * HALVES * P + u, (g + 1) * HALVES * P, HALVES)
+                nc.tensor.transpose(bank[:, g, u, :], words[:, every_second], identity[:])
+            return bank
+
+        def transpose_x(t):
+            bank = transpose_words(x_rows[t][:].bitcast(F32), PASSES * HALVES)
+            nc.scalar.copy(
+                out=x_grouped[t][:].bitcast(F32).rearrange("p (g c u) -> p g c u", g=PASSES, u=HALVES),
+                in_=bank[:].rearrange("p g u c -> p g c u"),
             )
 
-        transpose_and_regroup(nc, banks, x_rows[0][:], identity[:], word_view(x_grouped[0][:]))
-        masked_weight_tile(0)
-        bias_sum = sums.tile([P, O], F32, tag="sum")
-        nc.tensor.matmul(out=bias_sum[:], lhsT=ones[:], rhs=bias_rows[:], start=True, stop=True)
-        bias_all = keep.tile([P, O], F32)
-        nc.scalar.copy(out=bias_all[:], in_=bias_sum[:])
-        masked_weight_tile(1)
+        def transpose_last(g, copy):
+            bank = transpose_words(last_rows[g][:].bitcast(F32), HALVES)
+            grouped = x_grouped[3][:, g * K_PASS : (g + 1) * K_PASS].bitcast(F32).rearrange("p (c u) -> p c u", u=HALVES)
+            copy(out=grouped, in_=bank[:, 0].rearrange("p u c -> p c u"))
 
-        x_mx = [quantise(nc, x_pool, x_grouped[0][:], P)]
-        w_codes, w_scales = quantise(nc, keep, w_grouped[:], O)
-        for t in range(1, B_TILES):
-            transpose_and_regroup(nc, banks, x_rows[t][:], identity[:], word_view(x_grouped[t][:]))
-            x_mx.append(quantise(nc, x_pool, x_grouped[t][:], P))
+        def quantise_x(t):
+            nc.vector.quantize_mx(
+                out=x_codes[t][:].rearrange("p g c -> p (g c)").bitcast(FP8X4),
+                scales=x_scales[t][:].rearrange("p g c -> p (g c)"),
+                in_=x_grouped[t][:],
+            )
 
-        for t in range(B_TILES):
-            x_codes, x_scales = x_mx[t]
-            acc = sums.tile([P, O], F32, tag="sum")
+        def quantise_last(g):
+            nc.vector.quantize_mx(
+                out=x_codes[3][:, g, :].bitcast(FP8X4),
+                scales=x_scales[3][:, g, :],
+                in_=x_grouped[3][:, g * K_PASS : (g + 1) * K_PASS],
+            )
+
+        w_grouped = {}
+
+        masked = {}
+
+        def mask_weight(j):
+            for g in range(PASSES):
+                k_pass = slice(g * K_PASS, (g + 1) * K_PASS)
+                masked[j, g] = keep.tile([P, K_PASS], BF16, name=f"masked{j}{g}")
+                nc.vector.tensor_mul(
+                    out=masked[j, g][:], in0=weight_rows[j][:, k_pass], in1=mask_rows[j][:, k_pass]
+                )
+
+        def transpose_weight(j):
+            for g in range(PASSES):
+                bank = transpose_words(masked[j, g][:].bitcast(F32), HALVES)
+                w_grouped[j, g] = keep.tile([P, K_PASS], BF16, align_bytes=64, name=f"w_grouped{j}{g}")
+                nc.scalar.copy(
+                    out=w_grouped[j, g][:].bitcast(F32).rearrange("p (c u) -> p c u", u=HALVES),
+                    in_=bank[:, 0].rearrange("p u c -> p c u"),
+                )
+
+        def quantise_w(j):
+            for g in range(PASSES):
+                nc.vector.quantize_mx(
+                    out=w_codes[:, g, j * P : (j + 1) * P].bitcast(FP8X4),
+                    scales=w_scales[:, g, j * P : (j + 1) * P],
+                    in_=w_grouped[j, g][:],
+                )
+
+        def multiply(t, acc):
             for g in range(PASSES):
                 nc.tensor.matmul_mx(
-                    out=acc[:],
-                    lhsT=x_codes[:, g, :].bitcast(FP8X4),
-                    lhsT_scale=x_scales[:, g, :],
+                    out=acc,
+                    lhsT=x_codes[t][:, g, :].bitcast(FP8X4),
+                    lhsT_scale=x_scales[t][:, g, :],
                     rhs=w_codes[:, g, :].bitcast(FP8X4),
                     rhs_scale=w_scales[:, g, :],
                     start=(g == 0),
                     stop=(g == PASSES - 1),
                 )
-            result = x_pool.tile([P, O], F32)
-            nc.vector.tensor_add(out=result[:], in0=acc[:], in1=bias_all[:])
+
+        def finish(t, acc):
+            result = keep.tile([P, O], F32, name=f"result{t}")
+            nc.vector.tensor_add(out=result[:], in0=acc, in1=bias_all[:])
             nc.sync.dma_start(out=out_tiles[t], in_=result[:])
+
+        transpose_x(0)
+        transpose_x(1)
+        mask_weight(0)
+        transpose_weight(0)
+        quantise_x(0)
+        mask_weight(1)
+        transpose_weight(1)
+        bias_sum = sums.tile([P, O], F32, tag="sum2")
+        nc.tensor.matmul(out=bias_sum[:], lhsT=ones[:], rhs=bias_rows[:], start=True, stop=True)
+        bias_all = keep.tile([P, O], F32)
+        quantise_x(1)
+        quantise_w(0)
+        transpose_x(2)
+        quantise_w(1)
+        transpose_last(0, nc.vector.tensor_copy)
+        transpose_last(1, nc.scalar.copy)
+        nc.scalar.copy(out=bias_all[:], in_=bias_sum[:])
+        acc = sums.tile([P, 2, O], F32, tag="sum01")
+        multiply(0, acc[:, 0, :])
+        multiply(1, acc[:, 1, :])
+        both = keep.tile([P, 2, O], F32)
+        quantise_x(2)
+        quantise_last(0)
+        quantise_last(1)
+        acc2 = sums.tile([P, O], F32, tag="sum2")
+        multiply(2, acc2[:])
+        acc3 = sums.tile([P, O], F32, tag="sum3")
+        multiply(3, acc3[:])
+        nc.vector.tensor_add(out=both[:], in0=acc[:], in1=bias_all[:].unsqueeze(1).to_broadcast([P, 2, O]))
+        nc.sync.dma_start(out=out.rearrange("(p t) o -> p t o", t=B_TILES)[:, 0:2, :], in_=both[:])
+        finish(2, acc2[:])
+        finish(3, acc3[:])

@@ -36,9 +36,11 @@ def tile_skeletonlinear_s_kernel(tc, x, weight, mask, bias, out):
         sums = ctx.enter_context(tc.psum_pool(name="sums", bufs=1))
         ctx.enter_context(tc.manual_schedule())
 
+        idle = keep.tile([P, O], F32)
+        nc.vector.memset(idle[:], 0.0)
         bias_rows = keep.tile([P, O], BF16)
         nc.vector.memset(bias_rows[:], 0.0)
-        ones = keep.tile([P, P], BF16)
+        ones = keep.tile([P, P], F32)
         nc.vector.memset(ones[:], 1.0)
         identity = keep.tile([P, P], F32)
         make_identity(nc, identity[:])
@@ -49,6 +51,7 @@ def tile_skeletonlinear_s_kernel(tc, x, weight, mask, bias, out):
             return rows
 
         x_rows = {t: load(x_tiles[t], f"x{t}") for t in (0, 1)}
+        nc.sync.dma_start(out=bias_rows[0:1, :], in_=bias.unsqueeze(0))
         weight_rows = {}
         mask_rows = {}
         for j in range(O_TILES):
@@ -56,7 +59,6 @@ def tile_skeletonlinear_s_kernel(tc, x, weight, mask, bias, out):
             mask_rows[j] = load(mask_tiles[j], f"mask{j}")
         x_rows[2] = load(x_tiles[2], "x2")
         last_rows = [load(x_tiles[3][:, g * K_PASS : (g + 1) * K_PASS], f"last{g}") for g in range(PASSES)]
-        nc.scalar.dma_start(out=bias_rows[0:1, :], in_=bias.unsqueeze(0))
 
         x_grouped = {}
         x_codes = {}
@@ -150,21 +152,25 @@ def tile_skeletonlinear_s_kernel(tc, x, weight, mask, bias, out):
 
         transpose_x(0)
         transpose_x(1)
+        bias_f32 = keep.tile([P, O], F32)
+        nc.vector.tensor_copy(out=bias_f32[:], in_=bias_rows[:])
+        bias_sum = sums.tile([P, O], F32, tag="sum2")
+        nc.tensor.matmul(out=bias_sum[:], lhsT=ones[:], rhs=bias_f32[:], start=True, stop=True)
+        bias_all = keep.tile([P, O], F32)
         mask_weight(0)
         transpose_weight(0)
         quantise_x(0)
+        unread = sums.tile([P, O], F32, tag="sum3")
+        nc.tensor.matmul(out=unread[:], lhsT=idle[:, :P], rhs=idle[:], start=True, stop=True)
+        nc.scalar.copy(out=bias_all[:], in_=bias_sum[:])
         mask_weight(1)
         transpose_weight(1)
-        bias_sum = sums.tile([P, O], F32, tag="sum2")
-        nc.tensor.matmul(out=bias_sum[:], lhsT=ones[:], rhs=bias_rows[:], start=True, stop=True)
-        bias_all = keep.tile([P, O], F32)
         quantise_x(1)
         quantise_w(0)
         transpose_x(2)
         quantise_w(1)
         transpose_last(0, nc.vector.tensor_copy)
         transpose_last(1, nc.scalar.copy)
-        nc.scalar.copy(out=bias_all[:], in_=bias_sum[:])
         acc = sums.tile([P, 2, O], F32, tag="sum01")
         multiply(0, acc[:, 0, :])
         multiply(1, acc[:, 1, :])

@@ -32,15 +32,13 @@ def tile_skeletonlinear_s_kernel(tc, x, weight, mask, bias, out):
     with ExitStack() as ctx:
         keep = ctx.enter_context(tc.tile_pool(name="keep", bufs=1))
         loads = ctx.enter_context(tc.tile_pool(name="loads", bufs=1))
-        banks = ctx.enter_context(tc.psum_pool(name="banks", bufs=5))
+        banks = ctx.enter_context(tc.psum_pool(name="banks", bufs=4))
         sums = ctx.enter_context(tc.psum_pool(name="sums", bufs=1))
         ctx.enter_context(tc.manual_schedule())
 
-        idle = keep.tile([P, O], F32)
-        nc.vector.memset(idle[:], 0.0)
         bias_rows = keep.tile([P, O], BF16)
         nc.vector.memset(bias_rows[:], 0.0)
-        ones = keep.tile([P, P], F32)
+        ones = keep.tile([P, P], BF16)
         nc.vector.memset(ones[:], 1.0)
         identity = keep.tile([P, P], F32)
         make_identity(nc, identity[:])
@@ -56,7 +54,13 @@ def tile_skeletonlinear_s_kernel(tc, x, weight, mask, bias, out):
         mask_rows = {}
         for j in range(O_TILES):
             weight_rows[j] = load(weight_tiles[j], f"weight{j}")
-            mask_rows[j] = load(mask_tiles[j], f"mask{j}")
+            if j == 0:
+                mask_rows[j] = load(mask_tiles[j], f"mask{j}")
+            else:
+                mask_rows[j] = loads.tile([P, K], BF16, name=f"mask{j}")
+                for g in range(PASSES):
+                    k_pass = slice(g * K_PASS, (g + 1) * K_PASS)
+                    nc.sync.dma_start(out=mask_rows[j][:, k_pass], in_=mask_tiles[j][:, k_pass])
         x_rows[2] = load(x_tiles[2], "x2")
         last_rows = [load(x_tiles[3][:, g * K_PASS : (g + 1) * K_PASS], f"last{g}") for g in range(PASSES)]
 
@@ -70,12 +74,15 @@ def tile_skeletonlinear_s_kernel(tc, x, weight, mask, bias, out):
         w_codes = keep.tile([P, PASSES, O], U32, align_bytes=64)
         w_scales = keep.tile([P, PASSES, O], U8, align_bytes=64)
 
-        def transpose_words(words, squares):
+        def transpose_words(words, squares, step=HALVES):
             bank = banks.tile([P, squares // HALVES, HALVES, P], F32, tag="bank")
             for s in range(squares):
                 g, u = divmod(s, HALVES)
-                every_second = slice(g * HALVES * P + u, (g + 1) * HALVES * P, HALVES)
-                nc.tensor.transpose(bank[:, g, u, :], words[:, every_second], identity[:])
+                if step == 1:
+                    square = slice(s * P, (s + 1) * P)
+                else:
+                    square = slice(g * HALVES * P + u, (g + 1) * HALVES * P, HALVES)
+                nc.tensor.transpose(bank[:, g, u, :], words[:, square], identity[:])
             return bank
 
         def transpose_x(t):
@@ -113,12 +120,14 @@ def tile_skeletonlinear_s_kernel(tc, x, weight, mask, bias, out):
                 k_pass = slice(g * K_PASS, (g + 1) * K_PASS)
                 masked[j, g] = keep.tile([P, K_PASS], BF16, name=f"masked{j}{g}")
                 nc.vector.tensor_mul(
-                    out=masked[j, g][:], in0=weight_rows[j][:, k_pass], in1=mask_rows[j][:, k_pass]
+                    out=masked[j, g][:].rearrange("r (u p e) -> r u p e", u=HALVES, e=2),
+                    in0=weight_rows[j][:, k_pass].rearrange("r (p u e) -> r u p e", u=HALVES, e=2),
+                    in1=mask_rows[j][:, k_pass].rearrange("r (p u e) -> r u p e", u=HALVES, e=2),
                 )
 
         def transpose_weight(j):
             for g in range(PASSES):
-                bank = transpose_words(masked[j, g][:].bitcast(F32), HALVES)
+                bank = transpose_words(masked[j, g][:].bitcast(F32), HALVES, step=1)
                 w_grouped[j, g] = keep.tile([P, K_PASS], BF16, align_bytes=64, name=f"w_grouped{j}{g}")
                 nc.scalar.copy(
                     out=w_grouped[j, g][:].bitcast(F32).rearrange("p (c u) -> p c u", u=HALVES),
@@ -152,16 +161,12 @@ def tile_skeletonlinear_s_kernel(tc, x, weight, mask, bias, out):
 
         transpose_x(0)
         transpose_x(1)
-        bias_f32 = keep.tile([P, O], F32)
-        nc.vector.tensor_copy(out=bias_f32[:], in_=bias_rows[:])
         bias_sum = sums.tile([P, O], F32, tag="sum2")
-        nc.tensor.matmul(out=bias_sum[:], lhsT=ones[:], rhs=bias_f32[:], start=True, stop=True)
+        nc.tensor.matmul(out=bias_sum[:], lhsT=ones[:], rhs=bias_rows[:], start=True, stop=True)
         bias_all = keep.tile([P, O], F32)
         mask_weight(0)
         transpose_weight(0)
         quantise_x(0)
-        unread = sums.tile([P, O], F32, tag="sum3")
-        nc.tensor.matmul(out=unread[:], lhsT=idle[:, :P], rhs=idle[:], start=True, stop=True)
         nc.scalar.copy(out=bias_all[:], in_=bias_sum[:])
         mask_weight(1)
         transpose_weight(1)
@@ -171,18 +176,13 @@ def tile_skeletonlinear_s_kernel(tc, x, weight, mask, bias, out):
         quantise_w(1)
         transpose_last(0, nc.vector.tensor_copy)
         transpose_last(1, nc.scalar.copy)
-        acc = sums.tile([P, 2, O], F32, tag="sum01")
-        multiply(0, acc[:, 0, :])
-        multiply(1, acc[:, 1, :])
-        both = keep.tile([P, 2, O], F32)
+        acc = [sums.tile([P, O], F32, tag=f"sum{t}", name=f"acc{t}") for t in range(B_TILES)]
+        multiply(0, acc[0][:])
+        multiply(1, acc[1][:])
         quantise_x(2)
         quantise_last(0)
         quantise_last(1)
-        acc2 = sums.tile([P, O], F32, tag="sum2")
-        multiply(2, acc2[:])
-        acc3 = sums.tile([P, O], F32, tag="sum3")
-        multiply(3, acc3[:])
-        nc.vector.tensor_add(out=both[:], in0=acc[:], in1=bias_all[:].unsqueeze(1).to_broadcast([P, 2, O]))
-        nc.sync.dma_start(out=out.rearrange("(p t) o -> p t o", t=B_TILES)[:, 0:2, :], in_=both[:])
-        finish(2, acc2[:])
-        finish(3, acc3[:])
+        multiply(2, acc[2][:])
+        multiply(3, acc[3][:])
+        for t in range(B_TILES):
+            finish(t, acc[t][:])

@@ -38,8 +38,10 @@ def tile_skeletonlinear_s_kernel(tc, x, weight, mask, bias, out):
 
         bias_rows = keep.tile([P, O], BF16)
         nc.vector.memset(bias_rows[:], 0.0)
-        ones = keep.tile([P, P], BF16)
+        ones = keep.tile([P, P], F32)
         nc.vector.memset(ones[:], 1.0)
+        idle = keep.tile([P, O], F32)
+        nc.vector.memset(idle[:], 0.0)
         identity = keep.tile([P, P], F32)
         make_identity(nc, identity[:])
 
@@ -48,7 +50,7 @@ def tile_skeletonlinear_s_kernel(tc, x, weight, mask, bias, out):
             nc.sync.dma_start(out=rows[:], in_=source)
             return rows
 
-        x_rows = {t: load(x_tiles[t], f"x{t}") for t in (0, 1)}
+        x_rows = {t: load(x_tiles[t], f"x{t}") for t in (0, 1, 2)}
         nc.sync.dma_start(out=bias_rows[0:1, :], in_=bias.unsqueeze(0))
         weight_rows = {}
         mask_rows = {}
@@ -61,7 +63,6 @@ def tile_skeletonlinear_s_kernel(tc, x, weight, mask, bias, out):
                 for g in range(PASSES):
                     k_pass = slice(g * K_PASS, (g + 1) * K_PASS)
                     nc.sync.dma_start(out=mask_rows[j][:, k_pass], in_=mask_tiles[j][:, k_pass])
-        x_rows[2] = load(x_tiles[2], "x2")
         last_rows = [load(x_tiles[3][:, g * K_PASS : (g + 1) * K_PASS], f"last{g}") for g in range(PASSES)]
 
         x_grouped = {}
@@ -160,29 +161,32 @@ def tile_skeletonlinear_s_kernel(tc, x, weight, mask, bias, out):
             nc.sync.dma_start(out=out_tiles[t], in_=result[:])
 
         transpose_x(0)
+        bias_f32 = keep.tile([P, O], F32)
+        nc.vector.tensor_copy(out=bias_f32[:], in_=bias_rows[:])
         transpose_x(1)
+        quantise_x(0)
+        transpose_x(2)
+        quantise_x(1)
         bias_sum = sums.tile([P, O], F32, tag="sum2")
-        nc.tensor.matmul(out=bias_sum[:], lhsT=ones[:], rhs=bias_rows[:], start=True, stop=True)
+        nc.tensor.matmul(out=bias_sum[:], lhsT=ones[:], rhs=bias_f32[:], start=True, stop=True)
         bias_all = keep.tile([P, O], F32)
+        nc.scalar.copy(out=bias_all[:], in_=bias_sum[:])
         mask_weight(0)
         transpose_weight(0)
-        quantise_x(0)
-        nc.scalar.copy(out=bias_all[:], in_=bias_sum[:])
+        quantise_x(2)
+        unread = sums.tile([P, O], F32, tag="sum3")
+        nc.tensor.matmul(out=unread[:], lhsT=idle[:, :P], rhs=idle[:], start=True, stop=True)
         mask_weight(1)
         transpose_weight(1)
-        quantise_x(1)
         quantise_w(0)
-        transpose_x(2)
         quantise_w(1)
-        transpose_last(0, nc.vector.tensor_copy)
+        transpose_last(0, nc.scalar.copy)
         transpose_last(1, nc.scalar.copy)
         acc = [sums.tile([P, O], F32, tag=f"sum{t}", name=f"acc{t}") for t in range(B_TILES)]
-        multiply(0, acc[0][:])
-        multiply(1, acc[1][:])
-        quantise_x(2)
+        for t in range(3):
+            multiply(t, acc[t][:])
         quantise_last(0)
         quantise_last(1)
-        multiply(2, acc[2][:])
         multiply(3, acc[3][:])
         for t in range(B_TILES):
             finish(t, acc[t][:])

@@ -50,7 +50,7 @@ def tile_skeletonlinear_s_kernel(tc, x, weight, mask, bias, out):
             nc.sync.dma_start(out=rows[:], in_=source)
             return rows
 
-        x_rows = {t: load(x_tiles[t], f"x{t}") for t in (0, 1, 2)}
+        x_rows = {0: load(x_tiles[0], "x0")}
         nc.sync.dma_start(out=bias_rows[0:1, :], in_=bias.unsqueeze(0))
         weight_rows = {}
         mask_rows = {}
@@ -63,6 +63,8 @@ def tile_skeletonlinear_s_kernel(tc, x, weight, mask, bias, out):
                 for g in range(PASSES):
                     k_pass = slice(g * K_PASS, (g + 1) * K_PASS)
                     nc.sync.dma_start(out=mask_rows[j][:, k_pass], in_=mask_tiles[j][:, k_pass])
+        for t in (1, 2):
+            x_rows[t] = load(x_tiles[t], f"x{t}")
         last_rows = [load(x_tiles[3][:, g * K_PASS : (g + 1) * K_PASS], f"last{g}") for g in range(PASSES)]
 
         x_grouped = {}
@@ -163,30 +165,32 @@ def tile_skeletonlinear_s_kernel(tc, x, weight, mask, bias, out):
         transpose_x(0)
         bias_f32 = keep.tile([P, O], F32)
         nc.vector.tensor_copy(out=bias_f32[:], in_=bias_rows[:])
-        transpose_x(1)
-        quantise_x(0)
-        transpose_x(2)
-        quantise_x(1)
         bias_sum = sums.tile([P, O], F32, tag="sum2")
         nc.tensor.matmul(out=bias_sum[:], lhsT=ones[:], rhs=bias_f32[:], start=True, stop=True)
         bias_all = keep.tile([P, O], F32)
-        nc.scalar.copy(out=bias_all[:], in_=bias_sum[:])
         mask_weight(0)
         transpose_weight(0)
-        quantise_x(2)
+        quantise_x(0)
         unread = sums.tile([P, O], F32, tag="sum3")
         nc.tensor.matmul(out=unread[:], lhsT=idle[:, :P], rhs=idle[:], start=True, stop=True)
+        nc.scalar.copy(out=bias_all[:], in_=bias_sum[:])
         mask_weight(1)
         transpose_weight(1)
         quantise_w(0)
+        transpose_x(1)
         quantise_w(1)
+        transpose_x(2)
+        acc = [sums.tile([P, O], F32, tag=f"sum{t}", name=f"acc{t}") for t in range(B_TILES)]
+        multiply(0, acc[0][:])
+        quantise_x(1)
+        finish(0, acc[0][:])
         transpose_last(0, nc.scalar.copy)
         transpose_last(1, nc.scalar.copy)
-        acc = [sums.tile([P, O], F32, tag=f"sum{t}", name=f"acc{t}") for t in range(B_TILES)]
-        for t in range(3):
-            multiply(t, acc[t][:])
+        quantise_x(2)
+        multiply(1, acc[1][:])
+        multiply(2, acc[2][:])
         quantise_last(0)
         quantise_last(1)
         multiply(3, acc[3][:])
-        for t in range(B_TILES):
+        for t in range(1, B_TILES):
             finish(t, acc[t][:])

from contextlib import ExitStack

import concourse.mybir as mybir
from concourse.masks import make_identity

F32 = mybir.dt.float32
BF16 = mybir.dt.bfloat16
U32 = mybir.dt.uint32
U8 = mybir.dt.uint8
FP8X4 = mybir.dt.float8_e4m3fn_x4

P = 128
PACK = 4
K_PASS = P * PACK
HALVES = 2

B, K, O = 512, 1024, 256
PASSES = K // K_PASS
B_TILES = B // P
O_TILES = O // P

FLOPS = 2 * B * K * O


def tile_skeletonlinear_s_kernel(tc, x, weight, mask, bias, out):
    nc = tc.nc
    x_tiles = x.rearrange("(p t) k -> t p k", t=B_TILES)
    out_tiles = out.rearrange("(p t) o -> t p o", t=B_TILES)
    weight_tiles = weight.rearrange("(j p) k -> j p k", p=P)
    mask_tiles = mask.rearrange("(j p) k -> j p k", p=P)

    with ExitStack() as ctx:
        keep = ctx.enter_context(tc.tile_pool(name="keep", bufs=1))
        loads = ctx.enter_context(tc.tile_pool(name="loads", bufs=1))
        banks = ctx.enter_context(tc.psum_pool(name="banks", bufs=4))
        sums = ctx.enter_context(tc.psum_pool(name="sums", bufs=1))
        ctx.enter_context(tc.manual_schedule())

        bias_rows = keep.tile([P, O], BF16)
        nc.vector.memset(bias_rows[:], 0.0)
        ones = keep.tile([P, P], F32)
        nc.vector.memset(ones[:], 1.0)
        idle = keep.tile([P, O], F32)
        nc.vector.memset(idle[:], 0.0)
        identity = keep.tile([P, P], F32)
        make_identity(nc, identity[:])

        def load(source, label):
            rows = loads.tile([P, source.shape[1]], BF16, name=label)
            nc.sync.dma_start(out=rows[:], in_=source)
            return rows

        x_rows = {0: load(x_tiles[0], "x0")}
        nc.sync.dma_start(out=bias_rows[0:1, :], in_=bias.unsqueeze(0))
        weight_rows = {}
        mask_rows = {}
        for j in range(O_TILES):
            weight_rows[j] = load(weight_tiles[j], f"weight{j}")
            if j == 0:
                mask_rows[j] = load(mask_tiles[j], f"mask{j}")
            else:
                mask_rows[j] = loads.tile([P, K], BF16, name=f"mask{j}")
                for g in range(PASSES):
                    k_pass = slice(g * K_PASS, (g + 1) * K_PASS)
                    nc.sync.dma_start(out=mask_rows[j][:, k_pass], in_=mask_tiles[j][:, k_pass])
        for t in (1, 2):
            x_rows[t] = load(x_tiles[t], f"x{t}")
        last_rows = [load(x_tiles[3][:, g * K_PASS : (g + 1) * K_PASS], f"last{g}") for g in range(PASSES)]

        x_grouped = {}
        x_codes = {}
        x_scales = {}
        for t in range(B_TILES):
            x_grouped[t] = keep.tile([P, PASSES * P * PACK], BF16, align_bytes=64, name=f"x_grouped{t}")
            x_codes[t] = keep.tile([P, PASSES, P], U32, align_bytes=64, name=f"x_codes{t}")
            x_scales[t] = keep.tile([P, PASSES, P], U8, align_bytes=64, name=f"x_scales{t}")
        w_codes = keep.tile([P, PASSES, O], U32, align_bytes=64)
        w_scales = keep.tile([P, PASSES, O], U8, align_bytes=64)

        def transpose_words(words, squares, step=HALVES):
            bank = banks.tile([P, squares // HALVES, HALVES, P], F32, tag="bank")
            for s in range(squares):
                g, u = divmod(s, HALVES)
                if step == 1:
                    square = slice(s * P, (s + 1) * P)
                else:
                    square = slice(g * HALVES * P + u, (g + 1) * HALVES * P, HALVES)
                nc.tensor.transpose(bank[:, g, u, :], words[:, square], identity[:])
            return bank

        def transpose_x(t):
            bank = transpose_words(x_rows[t][:].bitcast(F32), PASSES * HALVES)
            nc.scalar.copy(
                out=x_grouped[t][:].bitcast(F32).rearrange("p (g c u) -> p g c u", g=PASSES, u=HALVES),
                in_=bank[:].rearrange("p g u c -> p g c u"),
            )

        def transpose_last(g, copy):
            bank = transpose_words(last_rows[g][:].bitcast(F32), HALVES)
            grouped = x_grouped[3][:, g * K_PASS : (g + 1) * K_PASS].bitcast(F32).rearrange("p (c u) -> p c u", u=HALVES)
            copy(out=grouped, in_=bank[:, 0].rearrange("p u c -> p c u"))

        def quantise_x(t):
            nc.vector.quantize_mx(
                out=x_codes[t][:].rearrange("p g c -> p (g c)").bitcast(FP8X4),
                scales=x_scales[t][:].rearrange("p g c -> p (g c)"),
                in_=x_grouped[t][:],
            )

        def quantise_last(g):
            nc.vector.quantize_mx(
                out=x_codes[3][:, g, :].bitcast(FP8X4),
                scales=x_scales[3][:, g, :],
                in_=x_grouped[3][:, g * K_PASS : (g + 1) * K_PASS],
            )

        w_grouped = {}

        masked = {}

        def mask_weight(j):
            for g in range(PASSES):
                k_pass = slice(g * K_PASS, (g + 1) * K_PASS)
                masked[j, g] = keep.tile([P, K_PASS], BF16, name=f"masked{j}{g}")
                nc.vector.tensor_mul(
                    out=masked[j, g][:].rearrange("r (u p e) -> r u p e", u=HALVES, e=2),
                    in0=weight_rows[j][:, k_pass].rearrange("r (p u e) -> r u p e", u=HALVES, e=2),
                    in1=mask_rows[j][:, k_pass].rearrange("r (p u e) -> r u p e", u=HALVES, e=2),
                )

        def transpose_weight(j):
            for g in range(PASSES):
                bank = transpose_words(masked[j, g][:].bitcast(F32), HALVES, step=1)
                w_grouped[j, g] = keep.tile([P, K_PASS], BF16, align_bytes=64, name=f"w_grouped{j}{g}")
                nc.scalar.copy(
                    out=w_grouped[j, g][:].bitcast(F32).rearrange("p (c u) -> p c u", u=HALVES),
                    in_=bank[:, 0].rearrange("p u c -> p c u"),
                )

        def quantise_w(j):
            for g in range(PASSES):
                nc.vector.quantize_mx(
                    out=w_codes[:, g, j * P : (j + 1) * P].bitcast(FP8X4),
                    scales=w_scales[:, g, j * P : (j + 1) * P],
                    in_=w_grouped[j, g][:],
                )

        def multiply(t, acc):
            for g in range(PASSES):
                nc.tensor.matmul_mx(
                    out=acc,
                    lhsT=x_codes[t][:, g, :].bitcast(FP8X4),
                    lhsT_scale=x_scales[t][:, g, :],
                    rhs=w_codes[:, g, :].bitcast(FP8X4),
                    rhs_scale=w_scales[:, g, :],
                    start=(g == 0),
                    stop=(g == PASSES - 1),
                )

        def finish(t, acc):
            result = keep.tile([P, O], F32, name=f"result{t}")
            nc.vector.tensor_add(out=result[:], in0=acc, in1=bias_all[:])
            nc.sync.dma_start(out=out_tiles[t], in_=result[:])

        transpose_x(0)
        bias_f32 = keep.tile([P, O], F32)
        nc.vector.tensor_copy(out=bias_f32[:], in_=bias_rows[:])
        bias_sum = sums.tile([P, O], F32, tag="sum2")
        nc.tensor.matmul(out=bias_sum[:], lhsT=ones[:], rhs=bias_f32[:], start=True, stop=True)
        bias_all = keep.tile([P, O], F32)
        mask_weight(0)
        transpose_weight(0)
        quantise_x(0)
        unread = sums.tile([P, O], F32, tag="sum3")
        nc.tensor.matmul(out=unread[:], lhsT=idle[:, :P], rhs=idle[:], start=True, stop=True)
        nc.scalar.copy(out=bias_all[:], in_=bias_sum[:])
        mask_weight(1)
        transpose_weight(1)
        quantise_w(0)
        transpose_x(1)
        quantise_w(1)
        transpose_x(2)
        acc = [sums.tile([P, O], F32, tag=f"sum{t}", name=f"acc{t}") for t in range(B_TILES)]
        multiply(0, acc[0][:])
        quantise_x(1)
        finish(0, acc[0][:])
        transpose_last(0, nc.scalar.copy)
        transpose_last(1, nc.scalar.copy)
        quantise_x(2)
        multiply(1, acc[1][:])
        multiply(2, acc[2][:])
        quantise_last(0)
        quantise_last(1)
        multiply(3, acc[3][:])
        for t in range(1, B_TILES):
            finish(t, acc[t][:])
